import numpy as np
import ml_dtypes


def mxq(x, axis, fmt="e4m3"):
    dtype, down = {"e4m3": (ml_dtypes.float8_e4m3fn, 7), "e5m2": (ml_dtypes.float8_e5m2, 14)}[fmt]
    v = np.moveaxis(np.asarray(x, np.float32).astype(ml_dtypes.bfloat16).astype(np.float64), axis, -1)
    blocks = v.reshape(v.shape[:-1] + (-1, 32))
    amax = np.abs(blocks).max(-1, keepdims=True)
    byte = np.maximum(np.where(amax > 0, np.frexp(amax)[1] - 1 + 127, 0) - down, 1)
    scale = np.exp2(byte - 127.0)
    codes = (blocks / scale).astype(np.float32).astype(dtype).astype(np.float64)
    return np.moveaxis((codes * scale).reshape(v.shape), -1, axis)


WIDE = False


def mx_kscale(k):
    if not WIDE:
        return np.ones(k)
    levels = np.array([18, -18])
    if k % 512:
        return np.exp2(np.random.permutation(np.resize(levels, k // 32))).repeat(32)
    a = np.empty((k // 512, 16))
    for p in range(k // 512):
        a[p, :8] = np.random.permutation(np.resize(levels, 8))
        for g in range(8):
            far = levels[np.abs(levels - a[p, g]) >= 10]
            a[p, g + 8] = far[np.random.randint(len(far))]
    return np.exp2(a.ravel()).repeat(32)


BF16 = ml_dtypes.bfloat16


def bf(x):
    return np.asarray(x, np.float32).astype(BF16)


def f64(x):
    return np.asarray(x).astype(np.float64)


B, C, D, T, H, W, P = 1, 1024, 512, 8, 16, 16, 2
N = T * H * W
NP = T * (H // P) * (W // P)


def setup_inputs():
    s = mx_kscale(N)[None, None, :]
    u = mx_kscale(D)[None, :, None]
    v = mx_kscale(NP)[None, None, :]
    theta0 = bf(np.random.standard_normal((B, D, N)) * 2.0)
    phi0 = bf(1.03 + 0.7 * np.random.standard_normal((B, D, NP)))
    g0 = bf(0.15 * (1.03 + 0.7 * np.random.standard_normal((B, D, NP))))
    grad = bf(4.0 * np.random.standard_normal((B, D, N)) * np.exp2(np.random.randint(-6, 1, (B, 1, N))) / s * u)
    f = (f64(theta0).transpose(0, 2, 1) @ f64(phi0)) / NP
    return {"theta_x": bf(f64(theta0) * s), "phi_x": bf(f64(phi0) / v), "g_x": bf(f64(g0) * v / u), "f": np.asarray(f, np.float32), "grad_out": grad}


def reference(theta_x, phi_x, g_x, f, grad_out):
    df = mxq(f64(grad_out), 1, "e5m2").transpose(0, 2, 1) @ mxq(f64(g_x), 1, "e4m3")
    dz = df / NP
    dtheta = mxq(f64(phi_x), 2, "e4m3") @ mxq(dz, 2, "e5m2").transpose(0, 2, 1)
    dphi = mxq(f64(theta_x), 2, "e4m3") @ mxq(dz, 1, "e5m2")
    return dtheta, dphi

@@ -1,0 +1,311 @@
+from contextlib import ExitStack
+
+import concourse.mybir as mybir
+from concourse.masks import make_identity
+
+D, N, M = 512, 2048, 512
+
+FLOPS = 3 * 2 * N * M * D
+BYTES = 2 * (2 * D * N + 2 * D * M) + 4 * (D * N + D * M)
+
+F32 = mybir.dt.float32
+BF16 = mybir.dt.bfloat16
+U32 = mybir.dt.uint32
+U8 = mybir.dt.uint8
+E4M3 = mybir.dt.float8_e4m3fn_x4
+E5M2 = mybir.dt.float8_e5m2_x4
+COPY = mybir.ActivationFunctionType.Copy
+MULT = mybir.AluOpType.mult
+
+P = 128
+PACK = 4
+GROUP = P * PACK
+GROUPS = N // GROUP
+TILES = D // P
+
+
+def tile_nonlocalblocknd_pb_v_kernel(tc, theta_x, phi_x, g_x, f, grad_out, out_0, out_1):
+    nc = tc.nc
+    theta, phi, g, grad = theta_x[0], phi_x[0], g_x[0], grad_out[0]
+    dtheta, dphi = out_0[0], out_1[0]
+
+    with ExitStack() as ctx:
+        sb = ctx.enter_context(tc.tile_pool(name="sb", bufs=1))
+        ps = ctx.enter_context(tc.psum_pool(name="ps", bufs=1))
+
+        def sbuf(name, shape, dtype):
+            return sb.tile(shape, dtype, name=name, tag=name, bufs=1, align_bytes=64)
+
+        def bank(name, tag, bufs, shape):
+            return ps.tile(shape, F32, name=name, tag=tag, bufs=bufs)
+
+        def copy_out(engine, out, in_):
+            if engine is nc.vector:
+                nc.vector.tensor_copy(out=out, in_=in_)
+            else:
+                nc.scalar.copy(out=out, in_=in_)
+
+        def mx(out, stat, stat_cols, mov, start, stop):
+            nc.tensor.matmul_mx(
+                out=out,
+                lhsT=stat[0][:, stat_cols].bitcast(E4M3),
+                lhsT_scale=stat[1][:, stat_cols],
+                rhs=mov[0][:].bitcast(E5M2),
+                rhs_scale=mov[1][:],
+                start=start,
+                stop=stop,
+            )
+
+        def codes(name, width):
+            return sbuf(name + "_codes", [P, width], U32), sbuf(name + "_scales", [P, width], U8)
+
+        def quantize(dst, cols, src, fmt):
+            nc.vector.quantize_mx(
+                out=dst[0][:, cols].bitcast(fmt),
+                scales=dst[1][:, cols],
+                in_=src[:, PACK * cols.start : PACK * cols.stop],
+            )
+
+        whole = slice(0, GROUP)
+
+        g_raw = sbuf("g_raw", [P, PACK, M], BF16)
+        g_grp = sbuf("g_grp", [P, PACK * M], BF16)
+        g_q = codes("g", M)
+        phi_raw = sbuf("phi_raw", [P, TILES, M], BF16)
+        phi_grp = sbuf("phi_grp", [P, PACK * D], BF16)
+        phi_q = codes("phi", D)
+        grad_raw = [sbuf("grad_raw%d" % i, [P, PACK, GROUP], BF16) for i in range(GROUPS)]
+        grad_grp = [sbuf("grad_grp%d" % i, [P, PACK * GROUP], BF16) for i in range(GROUPS)]
+        grad_q = [codes("grad%d" % i, GROUP) for i in range(GROUPS)]
+        dz = [sbuf("dz%d" % i, [P, PACK, GROUP], BF16) for i in range(GROUPS)]
+        a_grp = [sbuf("a_grp%d" % i, [P, PACK * GROUP], BF16) for i in range(GROUPS)]
+        a_q = [codes("a%d" % i, GROUP) for i in range(GROUPS)]
+        b_grp = [sbuf("b_grp%d" % i, [P, PACK * M], BF16) for i in range(GROUPS)]
+        b_q = [codes("b%d" % i, M) for i in range(GROUPS)]
+        th_raw = [sbuf("th_raw%d" % i, [P, N], BF16) for i in range(TILES)]
+        th_grp = [sbuf("th_grp%d" % i, [P, PACK * GROUP], BF16) for i in range(TILES)]
+        th_q = [codes("th%d" % i, GROUP) for i in range(TILES)]
+        o_sb = [sbuf("o_sb%d" % i, [P, TILES, GROUP], F32) for i in range(GROUPS)]
+        r_sb = sbuf("r_sb", [P, TILES, M], F32)
+        ident = sbuf("ident", [P, P], F32)
+        warm = sbuf("warm", [P, 1], F32)
+
+        def load_grad(G, c0, c1):
+            nc.sync.dma_start(
+                out=grad_raw[G][:, :, c0:c1],
+                in_=grad[:, G * GROUP + c0 : G * GROUP + c1].rearrange("(p j) n -> p j n", j=PACK),
+            )
+
+        def gi(engine, G, c0, c1):
+            copy_out(
+                engine,
+                grad_grp[G][:, PACK * c0 : PACK * c1].rearrange("p (w j) -> p w j", j=PACK),
+                grad_raw[G][:, :, c0:c1].rearrange("p j w -> p w j"),
+            )
+
+        def g_interleave(engine, h):
+            copy_out(
+                engine,
+                g_grp[:, 1024 * h : 1024 * (h + 1)].rearrange("p (s q j) -> p s q j", s=2, j=PACK),
+                g_raw[:].rearrange("p j (q s) -> p s q j", s=PACK)[:, 2 * h : 2 * h + 2, :, :],
+            )
+
+        df_banks = {}
+
+        def df(G, s):
+            acc = bank("df%d_%d" % (G, s), "df", 4, [P, GROUP])
+            mx(acc[:], g_q, slice(P * s, P * (s + 1)), grad_q[G], True, True)
+            df_banks[G, s] = acc
+
+        def de(engine, G, s):
+            out = dz[G][:, s, :].rearrange("q (u p e) -> q u p e", u=2, e=2)
+            in_ = df_banks[G, s][:].rearrange("q (p u e) -> q u p e", u=2, e=2)
+            if engine is nc.vector:
+                nc.vector.tensor_scalar(out=out, in0=in_, scalar1=1.0 / M, scalar2=None, op0=MULT)
+            else:
+                nc.scalar.activation(out=out, in_=in_, func=COPY, scale=1.0 / M)
+
+        def ai(G):
+            nc.vector.tensor_copy(
+                out=a_grp[G][:].rearrange("q (c s) -> q c s", s=PACK),
+                in_=dz[G][:].rearrange("q s c -> q c s"),
+            )
+
+        tr_banks = {}
+
+        def b_transposes(G, h):
+            tr = bank("bt%d_%d" % (G, h), "tr", 2, [P, 2, 2, P])
+            for i in range(2):
+                words = dz[G][:, 2 * h + i, :].bitcast(F32)
+                for u in range(2):
+                    nc.tensor.transpose(tr[:, i, u, :], words[:, P * u : P * (u + 1)], ident[:])
+            tr_banks["b", G, h] = tr
+
+        def be(engine, G, h):
+            copy_out(
+                engine,
+                b_grp[G][:, 1024 * h : 1024 * (h + 1)].bitcast(F32).rearrange("p (s q u) -> p s q u", s=2, u=2),
+                tr_banks["b", G, h][:].rearrange("p s u q -> p s q u"),
+            )
+
+        def phi_transposes(h):
+            tr = bank("pt%d" % h, "tr", 2, [P, 2, 2, P])
+            for i in range(2):
+                words = phi_raw[:, 2 * h + i, :].bitcast(F32)
+                for u in range(2):
+                    nc.tensor.transpose(tr[:, i, u, :], words[:, u::2], ident[:])
+            tr_banks["p", h] = tr
+
+        def pe(engine, h):
+            copy_out(
+                engine,
+                phi_grp[:, 1024 * h : 1024 * (h + 1)].bitcast(F32).rearrange("p (s q u) -> p s q u", s=2, u=2),
+                tr_banks["p", h][:].rearrange("p s u q -> p s q u"),
+            )
+
+        def th_transposes(i, h):
+            tr = bank("tt%d_%d" % (i, h), "tr", 2, [P, 2, 2, P])
+            words = th_raw[i][:].bitcast(F32)
+            for k in range(2):
+                w0 = 256 * (2 * h + k)
+                for u in range(2):
+                    nc.tensor.transpose(tr[:, k, u, :], words[:, w0 + u : w0 + 256 : 2], ident[:])
+            tr_banks["t", i, h] = tr
+
+        def te(engine, i, h):
+            copy_out(
+                engine,
+                th_grp[i][:, 1024 * h : 1024 * (h + 1)].bitcast(F32).rearrange("p (s q u) -> p s q u", s=2, u=2),
+                tr_banks["t", i, h][:].rearrange("p s u q -> p s q u"),
+            )
+
+        o_banks = {}
+
+        def o_mm(G, i):
+            acc = bank("o%d_%d" % (G, i), "o", 2, [P, GROUP])
+            mx(acc[:], phi_q, slice(P * i, P * (i + 1)), a_q[G], True, True)
+            o_banks[G, i] = acc
+
+        def oe(engine, G, i):
+            copy_out(
+                engine,
+                o_sb[G][:, i, :].rearrange("d (p u e) -> d p u e", u=2, e=2),
+                o_banks[G, i][:].rearrange("d (u p e) -> d p u e", u=2, e=2),
+            )
+            nc.sync.dma_start(
+                out=dtheta[P * i : P * (i + 1), GROUP * G : GROUP * (G + 1)], in_=o_sb[G][:, i, :]
+            )
+
+        r_banks = {}
+
+        def r_mm(i, G):
+            if G == 0:
+                r_banks[i] = bank("r%d" % i, "df", 4, [P, M])
+            mx(r_banks[i][:], th_q[i], slice(P * G, P * (G + 1)), b_q[G], G == 0, G == GROUPS - 1)
+
+        def re(engine, i):
+            copy_out(
+                engine,
+                r_sb[:, i, :].rearrange("d (q s) -> d q s", s=PACK),
+                r_banks[i][:].rearrange("d (s q) -> d q s", s=PACK),
+            )
+            nc.sync.dma_start(out=dphi[P * i : P * (i + 1), :], in_=r_sb[:, i, :])
+
+        V, S = nc.vector, nc.scalar
+        with tc.manual_schedule():
+            load_grad(0, 0, 256)
+            load_grad(0, 256, 512)
+            nc.sync.dma_start(out=g_raw[:], in_=g.rearrange("(p j) m -> p j m", j=PACK))
+            nc.sync.dma_start(out=phi_raw[:], in_=phi.rearrange("(i p) m -> p i m", p=P))
+            load_grad(1, 0, GROUP)
+            for i in range(TILES):
+                nc.sync.dma_start(out=th_raw[i][:], in_=theta[P * i : P * (i + 1), :])
+                if i + 2 < GROUPS:
+                    load_grad(i + 2, 0, GROUP)
+
+            nc.vector.memset(warm[:], 0.0)
+            nc.scalar.activation(out=warm[:], in_=warm[:], func=COPY, scale=1.0)
+            make_identity(nc, ident[:])
+
+            gi(V, 0, 0, 256)
+            gi(V, 0, 256, 384)
+            gi(S, 0, 384, 512)
+            quantize(grad_q[0], whole, grad_grp[0], E5M2)
+            g_interleave(V, 0)
+            g_interleave(S, 1)
+            quantize(g_q, slice(0, 256), g_grp, E4M3)
+            quantize(g_q, slice(256, 512), g_grp, E4M3)
+            df(0, 0)
+            df(0, 1)
+            phi_transposes(0)
+            df(0, 2)
+            df(0, 3)
+            phi_transposes(1)
+
+            th_of = {0: [0, 1], 1: [2], 2: [3], 3: []}
+            for G in range(GROUPS):
+                last = G == GROUPS - 1
+                if G == 0:
+                    pe(V, 0)
+                de(S, G, 0)
+                de(V if last else S, G, 1)
+                if not last:
+                    gi(V, G + 1, 0, GROUP)
+                if G > 0:
+                    o_mm(G - 1, 0)
+                    o_mm(G - 1, 1)
+                b_transposes(G, 0)
+                de(S, G, 2)
+                de(V if last else S, G, 3)
+                if G > 0:
+                    for i in th_of[G - 1]:
+                        quantize(th_q[i], whole, th_grp[i], E4M3)
+                    oe(V, G - 1, 0)
+                else:
+                    pe(V, 1)
+                if not last:
+                    quantize(grad_q[G + 1], whole, grad_grp[G + 1], E5M2)
+                be(S, G, 0)
+                if G > 0:
+                    o_mm(G - 1, 2)
+                b_transposes(G, 1)
+                ai(G)
+                if G > 0:
+                    oe(S, G - 1, 1)
+                else:
+                    quantize(phi_q, whole, phi_grp, E4M3)
+                be(S, G, 1)
+                if G > 0:
+                    o_mm(G - 1, 3)
+                    oe(S, G - 1, 2)
+                    oe(S, G - 1, 3)
+                for i in th_of[G]:
+                    for h in range(2):
+                        th_transposes(i, h)
+                        te(S, i, h)
+                if last:
+                    quantize(b_q[G], whole, b_grp[G], E5M2)
+                    quantize(a_q[G], whole, a_grp[G], E5M2)
+                else:
+                    quantize(a_q[G], whole, a_grp[G], E5M2)
+                    quantize(b_q[G], whole, b_grp[G], E5M2)
+                    for s in range(PACK):
+                        df(G + 1, s)
+
+            for i in range(TILES):
+                for G in range(GROUPS - 1):
+                    r_mm(i, G)
+            for i in range(TILES):
+                r_mm(i, GROUPS - 1)
+            re(S, 0)
+            re(V, 1)
+            o_mm(3, 0)
+            o_mm(3, 1)
+            re(S, 2)
+            re(V, 3)
+            oe(S, 3, 0)
+            oe(V, 3, 1)
+            o_mm(3, 2)
+            o_mm(3, 3)
+            oe(S, 3, 2)
+            oe(V, 3, 3)

@@ -113,7 +113,7 @@ def tile_nonlocalblocknd_pb_v_kernel(tc, theta_x, phi_x, g_x, f, grad_out, out_0
         df_banks = {}
 
         def df(G, s):
-            acc = bank("df%d_%d" % (G, s), "df", 4, [P, GROUP])
+            acc = bank("df%d_%d" % (G, s), "m", 6, [P, GROUP])
             mx(acc[:], g_q, slice(P * s, P * (s + 1)), grad_q[G], True, True)
             df_banks[G, s] = acc
 
@@ -134,7 +134,7 @@ def tile_nonlocalblocknd_pb_v_kernel(tc, theta_x, phi_x, g_x, f, grad_out, out_0
         tr_banks = {}
 
         def b_transposes(G, h):
-            tr = bank("bt%d_%d" % (G, h), "tr", 2, [P, 2, 2, P])
+            tr = bank("bt%d_%d" % (G, h), "m", 6, [P, 2, 2, P])
             for i in range(2):
                 words = dz[G][:, 2 * h + i, :].bitcast(F32)
                 for u in range(2):
@@ -149,7 +149,7 @@ def tile_nonlocalblocknd_pb_v_kernel(tc, theta_x, phi_x, g_x, f, grad_out, out_0
             )
 
         def phi_transposes(h):
-            tr = bank("pt%d" % h, "tr", 2, [P, 2, 2, P])
+            tr = bank("pt%d" % h, "m", 6, [P, 2, 2, P])
             for i in range(2):
                 words = phi_raw[:, 2 * h + i, :].bitcast(F32)
                 for u in range(2):
@@ -164,7 +164,7 @@ def tile_nonlocalblocknd_pb_v_kernel(tc, theta_x, phi_x, g_x, f, grad_out, out_0
             )
 
         def th_transposes(i, h):
-            tr = bank("tt%d_%d" % (i, h), "tr", 2, [P, 2, 2, P])
+            tr = bank("tt%d_%d" % (i, h), "m", 6, [P, 2, 2, P])
             words = th_raw[i][:].bitcast(F32)
             for k in range(2):
                 w0 = 256 * (2 * h + k)
@@ -182,7 +182,7 @@ def tile_nonlocalblocknd_pb_v_kernel(tc, theta_x, phi_x, g_x, f, grad_out, out_0
         o_banks = {}
 
         def o_mm(G, i):
-            acc = bank("o%d_%d" % (G, i), "o", 2, [P, GROUP])
+            acc = bank("o%d_%d" % (G, i), "m", 6, [P, GROUP])
             mx(acc[:], phi_q, slice(P * i, P * (i + 1)), a_q[G], True, True)
             o_banks[G, i] = acc
 
@@ -200,7 +200,7 @@ def tile_nonlocalblocknd_pb_v_kernel(tc, theta_x, phi_x, g_x, f, grad_out, out_0
 
         def r_mm(i, G):
             if G == 0:
-                r_banks[i] = bank("r%d" % i, "df", 4, [P, M])
+                r_banks[i] = bank("r%d" % i, "r", 2, [P, M])
             mx(r_banks[i][:], th_q[i], slice(P * G, P * (G + 1)), b_q[G], G == 0, G == GROUPS - 1)
 
         def re(engine, i):
@@ -241,71 +241,62 @@ def tile_nonlocalblocknd_pb_v_kernel(tc, theta_x, phi_x, g_x, f, grad_out, out_0
             df(0, 2)
             df(0, 3)
             phi_transposes(1)
-
-            th_of = {0: [0, 1], 1: [2], 2: [3], 3: []}
+            de(S, 0, 0)
+            de(S, 0, 1)
+            pe(V, 0)
+            gi(V, 1, 0, GROUP)
+            de(S, 0, 2)
+            de(S, 0, 3)
+            pe(S, 1)
+            quantize(grad_q[1], whole, grad_grp[1], E5M2)
+            voe = {1: [2], 2: [0,2], 3: [1,3]}
+            vde = {3: [3]}
+            th_of = {0: [0,1], 1: [2], 2: [], 3: [3]}
             for G in range(GROUPS):
-                last = G == GROUPS - 1
-                if G == 0:
-                    pe(V, 0)
-                de(S, G, 0)
-                de(V if last else S, G, 1)
-                if not last:
-                    gi(V, G + 1, 0, GROUP)
                 if G > 0:
-                    o_mm(G - 1, 0)
-                    o_mm(G - 1, 1)
+                    for i in range(4):
+                        o_mm(G - 1, i)
                 b_transposes(G, 0)
-                de(S, G, 2)
-                de(V if last else S, G, 3)
-                if G > 0:
-                    for i in th_of[G - 1]:
-                        quantize(th_q[i], whole, th_grp[i], E4M3)
-                    oe(V, G - 1, 0)
-                else:
-                    pe(V, 1)
-                if not last:
-                    quantize(grad_q[G + 1], whole, grad_grp[G + 1], E5M2)
-                be(S, G, 0)
-                if G > 0:
-                    o_mm(G - 1, 2)
                 b_transposes(G, 1)
-                ai(G)
-                if G > 0:
-                    oe(S, G - 1, 1)
-                else:
+                if G + 2 < GROUPS:
+                    gi(V, G + 2, 0, GROUP)
+                if G == 0:
                     quantize(phi_q, whole, phi_grp, E4M3)
-                be(S, G, 1)
                 if G > 0:
-                    o_mm(G - 1, 3)
-                    oe(S, G - 1, 2)
-                    oe(S, G - 1, 3)
+                    for i in range(4):
+                        oe(V if i in voe[G] else S, G - 1, i)
+                ai(G)
+                be(S, G, 0)
+                be(S, G, 1)
+                if G + 2 < GROUPS:
+                    quantize(grad_q[G + 2], whole, grad_grp[G + 2], E5M2)
                 for i in th_of[G]:
-                    for h in range(2):
-                        th_transposes(i, h)
-                        te(S, i, h)
-                if last:
-                    quantize(b_q[G], whole, b_grp[G], E5M2)
-                    quantize(a_q[G], whole, a_grp[G], E5M2)
-                else:
-                    quantize(a_q[G], whole, a_grp[G], E5M2)
-                    quantize(b_q[G], whole, b_grp[G], E5M2)
+                    th_transposes(i, 0)
+                    th_transposes(i, 1)
+                    te(S, i, 0)
+                    te(S, i, 1)
+                quantize(a_q[G], whole, a_grp[G], E5M2)
+                if G + 1 < GROUPS:
                     for s in range(PACK):
                         df(G + 1, s)
-
-            for i in range(TILES):
-                for G in range(GROUPS - 1):
-                    r_mm(i, G)
-            for i in range(TILES):
-                r_mm(i, GROUPS - 1)
-            re(S, 0)
-            re(V, 1)
-            o_mm(3, 0)
-            o_mm(3, 1)
-            re(S, 2)
-            re(V, 3)
-            oe(S, 3, 0)
-            oe(V, 3, 1)
-            o_mm(3, 2)
-            o_mm(3, 3)
-            oe(S, 3, 2)
-            oe(V, 3, 3)
+                    for s in range(PACK):
+                        de(V if s in vde.get(G + 1, []) else S, G + 1, s)
+                for i in th_of[G]:
+                    quantize(th_q[i], whole, th_grp[i], E4M3)
+                quantize(b_q[G], whole, b_grp[G], E5M2)
+                if G == 3:
+                    for i in range(2):
+                        for k in range(3):
+                            r_mm(i, k)
+            for i in range(4):
+                o_mm(3, i)
+            for i in range(2):
+                r_mm(i, 3)
+            for i, e in enumerate("SVSV"):
+                oe(V if e == "V" else S, 3, i)
+            for k in range(4):
+                r_mm(2, k)
+            for k in range(4):
+                r_mm(3, k)
+            for i, e in enumerate("SVSV"):
+                re(V if e == "V" else S, i)

@@ -21,11 +21,23 @@ P = 128
 PACK = 4
 GROUP = P * PACK
 GROUPS = N // GROUP
+LAST = GROUPS - 1
 TILES = D // P
+HALF = PACK * GROUP // 2
+WORDS = GROUP // 2
+
+HELD_BANKS = 2
+SHARED_BANKS = 8 - HELD_BANKS
+
+VECTOR_DZ = ((), (), (1,), (0, 2))
+VECTOR_OUT0 = (((1,), (), ()), ((0,), (3,), ()), ((), (), (0, 1)))
+VECTOR_OUT0_LAST = (3,)
+VECTOR_OUT1 = (1,)
 
 
 def tile_nonlocalblocknd_pb_v_kernel(tc, theta_x, phi_x, g_x, f, grad_out, out_0, out_1):
     nc = tc.nc
+    vector, scalar = nc.vector, nc.scalar
     theta, phi, g, grad = theta_x[0], phi_x[0], g_x[0], grad_out[0]
     dtheta, dphi = out_0[0], out_1[0]
 
@@ -36,267 +48,271 @@ def tile_nonlocalblocknd_pb_v_kernel(tc, theta_x, phi_x, g_x, f, grad_out, out_0
         def sbuf(name, shape, dtype):
             return sb.tile(shape, dtype, name=name, tag=name, bufs=1, align_bytes=64)
 
-        def bank(name, tag, bufs, shape):
-            return ps.tile(shape, F32, name=name, tag=tag, bufs=bufs)
+        def shared_bank(name, shape):
+            return ps.tile(shape, F32, name=name, tag="shared", bufs=SHARED_BANKS)
 
-        def copy_out(engine, out, in_):
-            if engine is nc.vector:
+        def held_bank(name):
+            return ps.tile([P, GROUP], F32, name=name, tag="held", bufs=HELD_BANKS)
+
+        def mx_tiles(name):
+            return sbuf(name + "_codes", [P, GROUP], U32), sbuf(name + "_scales", [P, GROUP], U8)
+
+        def four(make, name, *args):
+            return [make("%s%d" % (name, i), *args) for i in range(TILES)]
+
+        operand = [P, PACK * GROUP]
+
+        grad_raw = four(sbuf, "grad_raw", [P, PACK, GROUP], BF16)
+        g_raw = sbuf("g_raw", [P, PACK, M], BF16)
+        phi_raw = sbuf("phi_raw", [P, TILES, M], BF16)
+        theta_raw = four(sbuf, "theta_raw", [P, N], BF16)
+        dz = four(sbuf, "dz", [P, PACK, GROUP], BF16)
+        grad_lay, grad_mx = four(sbuf, "grad_lay", operand, BF16), four(mx_tiles, "grad")
+        g_lay, g_mx = sbuf("g_lay", operand, BF16), mx_tiles("g")
+        phi_lay, phi_mx = sbuf("phi_lay", operand, BF16), mx_tiles("phi")
+        theta_lay, theta_mx = four(sbuf, "theta_lay", operand, BF16), four(mx_tiles, "theta")
+        dzm_lay, dzm_mx = four(sbuf, "dzm_lay", operand, BF16), four(mx_tiles, "dzm")
+        dzn_lay, dzn_mx = four(sbuf, "dzn_lay", operand, BF16), four(mx_tiles, "dzn")
+        out0_sb = four(sbuf, "out0_sb", [P, TILES, GROUP], F32)
+        out1_sb = sbuf("out1_sb", [P, TILES, M], F32)
+
+        ident = sbuf("ident", [P, P], F32)
+        table = sbuf("table", [P, 1], F32)
+
+        dz_bank, word_bank, out0_bank, out1_bank = {}, {}, {}, {}
+
+
+        def copy(engine, out, in_):
+            if engine is vector:
                 nc.vector.tensor_copy(out=out, in_=in_)
             else:
                 nc.scalar.copy(out=out, in_=in_)
 
-        def mx(out, stat, stat_cols, mov, start, stop):
+        def quantize(mx, lay, fmt, cols=slice(0, GROUP)):
+            codes, scales = mx
+            nc.vector.quantize_mx(
+                out=codes[:, cols].bitcast(fmt),
+                scales=scales[:, cols],
+                in_=lay[:, PACK * cols.start : PACK * cols.stop],
+            )
+
+        def multiply(out, still, i, moving, start, stop):
+            cols = slice(P * i, P * (i + 1))
             nc.tensor.matmul_mx(
-                out=out,
-                lhsT=stat[0][:, stat_cols].bitcast(E4M3),
-                lhsT_scale=stat[1][:, stat_cols],
-                rhs=mov[0][:].bitcast(E5M2),
-                rhs_scale=mov[1][:],
+                out=out[:],
+                lhsT=still[0][:, cols].bitcast(E4M3),
+                lhsT_scale=still[1][:, cols],
+                rhs=moving[0][:].bitcast(E5M2),
+                rhs_scale=moving[1][:],
                 start=start,
                 stop=stop,
             )
 
-        def codes(name, width):
-            return sbuf(name + "_codes", [P, width], U32), sbuf(name + "_scales", [P, width], U8)
 
-        def quantize(dst, cols, src, fmt):
-            nc.vector.quantize_mx(
-                out=dst[0][:, cols].bitcast(fmt),
-                scales=dst[1][:, cols],
-                in_=src[:, PACK * cols.start : PACK * cols.stop],
-            )
-
-        whole = slice(0, GROUP)
-
-        g_raw = sbuf("g_raw", [P, PACK, M], BF16)
-        g_grp = sbuf("g_grp", [P, PACK * M], BF16)
-        g_q = codes("g", M)
-        phi_raw = sbuf("phi_raw", [P, TILES, M], BF16)
-        phi_grp = sbuf("phi_grp", [P, PACK * D], BF16)
-        phi_q = codes("phi", D)
-        grad_raw = [sbuf("grad_raw%d" % i, [P, PACK, GROUP], BF16) for i in range(GROUPS)]
-        grad_grp = [sbuf("grad_grp%d" % i, [P, PACK * GROUP], BF16) for i in range(GROUPS)]
-        grad_q = [codes("grad%d" % i, GROUP) for i in range(GROUPS)]
-        dz = [sbuf("dz%d" % i, [P, PACK, GROUP], BF16) for i in range(GROUPS)]
-        a_grp = [sbuf("a_grp%d" % i, [P, PACK * GROUP], BF16) for i in range(GROUPS)]
-        a_q = [codes("a%d" % i, GROUP) for i in range(GROUPS)]
-        b_grp = [sbuf("b_grp%d" % i, [P, PACK * M], BF16) for i in range(GROUPS)]
-        b_q = [codes("b%d" % i, M) for i in range(GROUPS)]
-        th_raw = [sbuf("th_raw%d" % i, [P, N], BF16) for i in range(TILES)]
-        th_grp = [sbuf("th_grp%d" % i, [P, PACK * GROUP], BF16) for i in range(TILES)]
-        th_q = [codes("th%d" % i, GROUP) for i in range(TILES)]
-        o_sb = [sbuf("o_sb%d" % i, [P, TILES, GROUP], F32) for i in range(GROUPS)]
-        r_sb = sbuf("r_sb", [P, TILES, M], F32)
-        ident = sbuf("ident", [P, P], F32)
-        warm = sbuf("warm", [P, 1], F32)
-
-        def load_grad(G, c0, c1):
+        def load_grad(G, first, last):
+            cols = grad[:, GROUP * G + first : GROUP * G + last]
             nc.sync.dma_start(
-                out=grad_raw[G][:, :, c0:c1],
-                in_=grad[:, G * GROUP + c0 : G * GROUP + c1].rearrange("(p j) n -> p j n", j=PACK),
+                out=grad_raw[G][:, :, first:last], in_=cols.rearrange("(p j) n -> p j n", j=PACK)
             )
 
-        def gi(engine, G, c0, c1):
-            copy_out(
+        def interleave_grad(engine, G, first, last):
+            copy(
                 engine,
-                grad_grp[G][:, PACK * c0 : PACK * c1].rearrange("p (w j) -> p w j", j=PACK),
-                grad_raw[G][:, :, c0:c1].rearrange("p j w -> p w j"),
+                grad_lay[G][:, PACK * first : PACK * last].rearrange("p (w i j) -> p w j i", i=4, j=PACK),
+                grad_raw[G][:, :, first:last].rearrange("p j (w i) -> p w j i", i=4),
             )
 
-        def g_interleave(engine, h):
-            copy_out(
+        def interleave_g(engine, half):
+            copy(
                 engine,
-                g_grp[:, 1024 * h : 1024 * (h + 1)].rearrange("p (s q j) -> p s q j", s=2, j=PACK),
-                g_raw[:].rearrange("p j (q s) -> p s q j", s=PACK)[:, 2 * h : 2 * h + 2, :, :],
+                g_lay[:, HALF * half : HALF * (half + 1)].rearrange("p (t q j) -> p t q j", t=2, j=PACK),
+                g_raw[:].rearrange("p j (q t) -> p t q j", t=PACK)[:, 2 * half : 2 * half + 2, :, :],
             )
 
-        df_banks = {}
+        def multiply_dz(G, t):
+            dz_bank[G, t] = shared_bank("dz_bank%d_%d" % (G, t), [P, GROUP])
+            multiply(dz_bank[G, t], g_mx, t, grad_mx[G], True, True)
 
-        def df(G, s):
-            acc = bank("df%d_%d" % (G, s), "m", 6, [P, GROUP])
-            mx(acc[:], g_q, slice(P * s, P * (s + 1)), grad_q[G], True, True)
-            df_banks[G, s] = acc
-
-        def de(engine, G, s):
-            out = dz[G][:, s, :].rearrange("q (u p e) -> q u p e", u=2, e=2)
-            in_ = df_banks[G, s][:].rearrange("q (p u e) -> q u p e", u=2, e=2)
-            if engine is nc.vector:
+        def copy_dz(G, t):
+            out = dz[G][:, t, :].rearrange("q (u p e) -> q u p e", u=2, e=2)
+            in_ = dz_bank[G, t][:].rearrange("q (p u e) -> q u p e", u=2, e=2)
+            if t in VECTOR_DZ[G]:
                 nc.vector.tensor_scalar(out=out, in0=in_, scalar1=1.0 / M, scalar2=None, op0=MULT)
             else:
                 nc.scalar.activation(out=out, in_=in_, func=COPY, scale=1.0 / M)
 
-        def ai(G):
+        def interleave_dz(G):
             nc.vector.tensor_copy(
-                out=a_grp[G][:].rearrange("q (c s) -> q c s", s=PACK),
-                in_=dz[G][:].rearrange("q s c -> q c s"),
+                out=dzm_lay[G][:].rearrange("q (c i t) -> q c t i", i=4, t=PACK),
+                in_=dz[G][:].rearrange("q t (c i) -> q c t i", i=4),
             )
 
-        tr_banks = {}
 
-        def b_transposes(G, h):
-            tr = bank("bt%d_%d" % (G, h), "m", 6, [P, 2, 2, P])
-            for i in range(2):
-                words = dz[G][:, 2 * h + i, :].bitcast(F32)
+        def transpose_words(key, blocks):
+            bank = shared_bank("words_%s_%d_%d" % key, [P, 2, 2, P])
+            for b, pair in enumerate(blocks):
                 for u in range(2):
-                    nc.tensor.transpose(tr[:, i, u, :], words[:, P * u : P * (u + 1)], ident[:])
-            tr_banks["b", G, h] = tr
+                    nc.tensor.transpose(bank[:, b, u, :], pair[u], ident[:])
+            word_bank[key] = bank
 
-        def be(engine, G, h):
-            copy_out(
-                engine,
-                b_grp[G][:, 1024 * h : 1024 * (h + 1)].bitcast(F32).rearrange("p (s q u) -> p s q u", s=2, u=2),
-                tr_banks["b", G, h][:].rearrange("p s u q -> p s q u"),
+        def copy_words(key, lay):
+            half = key[2]
+            nc.scalar.copy(
+                out=lay[:, HALF * half : HALF * (half + 1)]
+                .bitcast(F32)
+                .rearrange("p (b c u) -> p b c u", b=2, u=2),
+                in_=word_bank[key][:].rearrange("p b u c -> p b c u"),
             )
 
-        def phi_transposes(h):
-            tr = bank("pt%d" % h, "m", 6, [P, 2, 2, P])
-            for i in range(2):
-                words = phi_raw[:, 2 * h + i, :].bitcast(F32)
-                for u in range(2):
-                    nc.tensor.transpose(tr[:, i, u, :], words[:, u::2], ident[:])
-            tr_banks["p", h] = tr
+        def every_second_word(words, block):
+            return [words[:, WORDS * block + u : WORDS * (block + 1) : 2] for u in range(2)]
 
-        def pe(engine, h):
-            copy_out(
-                engine,
-                phi_grp[:, 1024 * h : 1024 * (h + 1)].bitcast(F32).rearrange("p (s q u) -> p s q u", s=2, u=2),
-                tr_banks["p", h][:].rearrange("p s u q -> p s q u"),
+        def transpose_phi(half):
+            transpose_words(
+                ("phi", 0, half),
+                [every_second_word(phi_raw[:, 2 * half + b, :].bitcast(F32), 0) for b in range(2)],
             )
 
-        def th_transposes(i, h):
-            tr = bank("tt%d_%d" % (i, h), "m", 6, [P, 2, 2, P])
-            words = th_raw[i][:].bitcast(F32)
-            for k in range(2):
-                w0 = 256 * (2 * h + k)
-                for u in range(2):
-                    nc.tensor.transpose(tr[:, k, u, :], words[:, w0 + u : w0 + 256 : 2], ident[:])
-            tr_banks["t", i, h] = tr
-
-        def te(engine, i, h):
-            copy_out(
-                engine,
-                th_grp[i][:, 1024 * h : 1024 * (h + 1)].bitcast(F32).rearrange("p (s q u) -> p s q u", s=2, u=2),
-                tr_banks["t", i, h][:].rearrange("p s u q -> p s q u"),
+        def transpose_theta(i, half):
+            transpose_words(
+                ("theta", i, half),
+                [every_second_word(theta_raw[i][:].bitcast(F32), 2 * half + b) for b in range(2)],
             )
 
-        o_banks = {}
+        def transpose_dz(G, half):
+            blocks = []
+            for b in range(2):
+                words = dz[G][:, 2 * half + b, :].bitcast(F32)
+                blocks.append([words[:, P * u : P * (u + 1)] for u in range(2)])
+            transpose_words(("dz", G, half), blocks)
 
-        def o_mm(G, i):
-            acc = bank("o%d_%d" % (G, i), "m", 6, [P, GROUP])
-            mx(acc[:], phi_q, slice(P * i, P * (i + 1)), a_q[G], True, True)
-            o_banks[G, i] = acc
 
-        def oe(engine, G, i):
-            copy_out(
+        def multiply_out0(G, i):
+            out0_bank[G, i] = shared_bank("out0_bank%d_%d" % (G, i), [P, GROUP])
+            multiply(out0_bank[G, i], phi_mx, i, dzm_mx[G], True, True)
+
+        def finish_out0(engine, G, i):
+            copy(
                 engine,
-                o_sb[G][:, i, :].rearrange("d (p u e) -> d p u e", u=2, e=2),
-                o_banks[G, i][:].rearrange("d (u p e) -> d p u e", u=2, e=2),
+                out0_sb[G][:, i, :].rearrange("d (p u e) -> d p u e", u=2, e=2),
+                out0_bank[G, i][:].rearrange("d (u p e) -> d p u e", u=2, e=2),
             )
             nc.sync.dma_start(
-                out=dtheta[P * i : P * (i + 1), GROUP * G : GROUP * (G + 1)], in_=o_sb[G][:, i, :]
+                out=dtheta[P * i : P * (i + 1), GROUP * G : GROUP * (G + 1)], in_=out0_sb[G][:, i, :]
             )
 
-        r_banks = {}
-
-        def r_mm(i, G):
+        def multiply_out1(i, G):
             if G == 0:
-                r_banks[i] = bank("r%d" % i, "r", 2, [P, M])
-            mx(r_banks[i][:], th_q[i], slice(P * G, P * (G + 1)), b_q[G], G == 0, G == GROUPS - 1)
+                name = "out1_bank%d" % i
+                out1_bank[i] = held_bank(name) if i < HELD_BANKS else shared_bank(name, [P, M])
+            multiply(out1_bank[i], theta_mx[i], G, dzn_mx[G], G == 0, G == LAST)
 
-        def re(engine, i):
-            copy_out(
+        def finish_out1(engine, i):
+            copy(
                 engine,
-                r_sb[:, i, :].rearrange("d (q s) -> d q s", s=PACK),
-                r_banks[i][:].rearrange("d (s q) -> d q s", s=PACK),
+                out1_sb[:, i, :].rearrange("d (q t) -> d q t", t=PACK),
+                out1_bank[i][:].rearrange("d (t q) -> d q t", t=PACK),
             )
-            nc.sync.dma_start(out=dphi[P * i : P * (i + 1), :], in_=r_sb[:, i, :])
+            nc.sync.dma_start(out=dphi[P * i : P * (i + 1), :], in_=out1_sb[:, i, :])
 
-        V, S = nc.vector, nc.scalar
+        def keep_warm(bank, times):
+            for i in range(times):
+                nc.tensor.matmul(
+                    out=bank[:], lhsT=grad_raw[0][:, 0, 0:P], rhs=grad_raw[0][:, 1, :], start=True, stop=True
+                )
+
         with tc.manual_schedule():
             load_grad(0, 0, 256)
-            load_grad(0, 256, 512)
+            load_grad(0, 256, GROUP)
             nc.sync.dma_start(out=g_raw[:], in_=g.rearrange("(p j) m -> p j m", j=PACK))
             nc.sync.dma_start(out=phi_raw[:], in_=phi.rearrange("(i p) m -> p i m", p=P))
             load_grad(1, 0, GROUP)
             for i in range(TILES):
-                nc.sync.dma_start(out=th_raw[i][:], in_=theta[P * i : P * (i + 1), :])
+                nc.sync.dma_start(out=theta_raw[i][:], in_=theta[P * i : P * (i + 1), :])
                 if i + 2 < GROUPS:
                     load_grad(i + 2, 0, GROUP)
 
-            nc.vector.memset(warm[:], 0.0)
-            nc.scalar.activation(out=warm[:], in_=warm[:], func=COPY, scale=1.0)
+            nc.vector.memset(table[:], 0.0)
+            nc.scalar.activation(out=table[:], in_=table[:], func=COPY, scale=1.0)
             make_identity(nc, ident[:])
 
-            gi(V, 0, 0, 256)
-            gi(V, 0, 256, 384)
-            gi(S, 0, 384, 512)
-            quantize(grad_q[0], whole, grad_grp[0], E5M2)
-            g_interleave(V, 0)
-            g_interleave(S, 1)
-            quantize(g_q, slice(0, 256), g_grp, E4M3)
-            quantize(g_q, slice(256, 512), g_grp, E4M3)
-            df(0, 0)
-            df(0, 1)
-            phi_transposes(0)
-            df(0, 2)
-            df(0, 3)
-            phi_transposes(1)
-            de(S, 0, 0)
-            de(S, 0, 1)
-            pe(V, 0)
-            gi(V, 1, 0, GROUP)
-            de(S, 0, 2)
-            de(S, 0, 3)
-            pe(S, 1)
-            quantize(grad_q[1], whole, grad_grp[1], E5M2)
-            voe = {1: [2], 2: [0,2], 3: [1,3]}
-            vde = {3: [3]}
-            th_of = {0: [0,1], 1: [2], 2: [], 3: [3]}
+            interleave_grad(vector, 0, 0, 256)
+            interleave_grad(vector, 0, 256, 384)
+            interleave_grad(scalar, 0, 384, GROUP)
+            quantize(grad_mx[0], grad_lay[0], E5M2)
+            interleave_g(vector, 0)
+            interleave_g(scalar, 1)
+            quantize(g_mx, g_lay, E4M3, slice(0, GROUP // 2))
+            quantize(g_mx, g_lay, E4M3, slice(GROUP // 2, GROUP))
+            unread_bank = held_bank("unread_bank")
+            keep_warm(unread_bank, 4)
+            multiply_dz(0, 0)
+            multiply_dz(0, 1)
+            transpose_phi(0)
+            multiply_dz(0, 2)
+            multiply_dz(0, 3)
+            transpose_phi(1)
+            keep_warm(unread_bank, 2)
+            copy_dz(0, 0)
+            copy_dz(0, 1)
+            copy_words(("phi", 0, 0), phi_lay)
+            interleave_grad(vector, 1, 0, GROUP)
+            copy_dz(0, 2)
+            copy_dz(0, 3)
+            copy_words(("phi", 0, 1), phi_lay)
+            quantize(grad_mx[1], grad_lay[1], E5M2)
+
             for G in range(GROUPS):
+                early, between, late = VECTOR_OUT0[G - 1] if G > 0 else ((), (), ())
                 if G > 0:
-                    for i in range(4):
-                        o_mm(G - 1, i)
-                b_transposes(G, 0)
-                b_transposes(G, 1)
+                    for i in range(TILES):
+                        multiply_out0(G - 1, i)
+                transpose_dz(G, 0)
+                transpose_dz(G, 1)
+                for i in range(HELD_BANKS):
+                    if G > i:
+                        for k in range(0 if G == i + 1 else G - 1, G):
+                            multiply_out1(i, k)
                 if G + 2 < GROUPS:
-                    gi(V, G + 2, 0, GROUP)
+                    interleave_grad(vector, G + 2, 0, GROUP)
                 if G == 0:
-                    quantize(phi_q, whole, phi_grp, E4M3)
+                    quantize(phi_mx, phi_lay, E4M3)
+                for i in early:
+                    finish_out0(vector, G - 1, i)
+                interleave_dz(G)
                 if G > 0:
-                    for i in range(4):
-                        oe(V if i in voe[G] else S, G - 1, i)
-                ai(G)
-                be(S, G, 0)
-                be(S, G, 1)
+                    for i in range(TILES):
+                        if i not in early + between + late:
+                            finish_out0(scalar, G - 1, i)
+                for i in between:
+                    finish_out0(vector, G - 1, i)
+                for half in range(2):
+                    copy_words(("dz", G, half), dzn_lay[G])
                 if G + 2 < GROUPS:
-                    quantize(grad_q[G + 2], whole, grad_grp[G + 2], E5M2)
-                for i in th_of[G]:
-                    th_transposes(i, 0)
-                    th_transposes(i, 1)
-                    te(S, i, 0)
-                    te(S, i, 1)
-                quantize(a_q[G], whole, a_grp[G], E5M2)
+                    quantize(grad_mx[G + 2], grad_lay[G + 2], E5M2)
+                for half in range(2):
+                    transpose_theta(G, half)
+                for half in range(2):
+                    copy_words(("theta", G, half), theta_lay[G])
+                quantize(dzm_mx[G], dzm_lay[G], E5M2)
+                for i in late:
+                    finish_out0(vector, G - 1, i)
                 if G + 1 < GROUPS:
-                    for s in range(PACK):
-                        df(G + 1, s)
-                    for s in range(PACK):
-                        de(V if s in vde.get(G + 1, []) else S, G + 1, s)
-                for i in th_of[G]:
-                    quantize(th_q[i], whole, th_grp[i], E4M3)
-                quantize(b_q[G], whole, b_grp[G], E5M2)
-                if G == 3:
-                    for i in range(2):
-                        for k in range(3):
-                            r_mm(i, k)
-            for i in range(4):
-                o_mm(3, i)
-            for i in range(2):
-                r_mm(i, 3)
-            for i, e in enumerate("SVSV"):
-                oe(V if e == "V" else S, 3, i)
-            for k in range(4):
-                r_mm(2, k)
-            for k in range(4):
-                r_mm(3, k)
-            for i, e in enumerate("SVSV"):
-                re(V if e == "V" else S, i)
+                    for t in range(PACK):
+                        multiply_dz(G + 1, t)
+                    for t in range(PACK):
+                        copy_dz(G + 1, t)
+                quantize(theta_mx[G], theta_lay[G], E4M3)
+                quantize(dzn_mx[G], dzn_lay[G], E5M2)
+
+            for i in range(TILES):
+                multiply_out0(LAST, i)
+            for i in range(TILES):
+                finish_out0(vector if i in VECTOR_OUT0_LAST else scalar, LAST, i)
+            for i in range(HELD_BANKS, TILES):
+                for G in range(LAST):
+                    multiply_out1(i, G)
+            for i in range(TILES):
+                multiply_out1(i, LAST)
+            for i in range(TILES):
+                finish_out1(vector if i in VECTOR_OUT1 else scalar, i)

@@ -29,10 +29,12 @@ WORDS = GROUP // 2
 HELD_BANKS = 2
 SHARED_BANKS = 8 - HELD_BANKS
 
-VECTOR_DZ = ((), (), (1,), (0, 2))
-VECTOR_OUT0 = (((1,), (), ()), ((0,), (3,), ()), ((), (), (0, 1)))
-VECTOR_OUT0_LAST = (3,)
-VECTOR_OUT1 = (1,)
+VECTOR_DZ = ((3,), (), (0, 2), (2,))
+VECTOR_WORDS = (("dz", 2, 1), ("theta", 2, 0), ("dz", 3, 1))
+VECTOR_OUT0 = (((2,), ()), ((), ()), ((), (1,)))
+VECTOR_OUT0_LAST = (2, 3)
+VECTOR_OUT1 = (2,)
+VECTOR_FIRST = 448
 
 
 def tile_nonlocalblocknd_pb_v_kernel(tc, theta_x, phi_x, g_x, f, grad_out, out_0, out_1):
@@ -157,11 +159,12 @@ def tile_nonlocalblocknd_pb_v_kernel(tc, theta_x, phi_x, g_x, f, grad_out, out_0
 
         def copy_words(key, lay):
             half = key[2]
-            nc.scalar.copy(
-                out=lay[:, HALF * half : HALF * (half + 1)]
+            copy(
+                vector if key in VECTOR_WORDS else scalar,
+                lay[:, HALF * half : HALF * (half + 1)]
                 .bitcast(F32)
                 .rearrange("p (b c u) -> p b c u", b=2, u=2),
-                in_=word_bank[key][:].rearrange("p b u c -> p b c u"),
+                word_bank[key][:].rearrange("p b u c -> p b c u"),
             )
 
         def every_second_word(words, block):
@@ -225,20 +228,20 @@ def tile_nonlocalblocknd_pb_v_kernel(tc, theta_x, phi_x, g_x, f, grad_out, out_0
             load_grad(0, 0, 256)
             load_grad(0, 256, GROUP)
             nc.sync.dma_start(out=g_raw[:], in_=g.rearrange("(p j) m -> p j m", j=PACK))
-            nc.sync.dma_start(out=phi_raw[:], in_=phi.rearrange("(i p) m -> p i m", p=P))
             load_grad(1, 0, GROUP)
+            nc.sync.dma_start(out=phi_raw[:], in_=phi.rearrange("(i p) m -> p i m", p=P))
             for i in range(TILES):
-                nc.sync.dma_start(out=theta_raw[i][:], in_=theta[P * i : P * (i + 1), :])
                 if i + 2 < GROUPS:
                     load_grad(i + 2, 0, GROUP)
+                nc.sync.dma_start(out=theta_raw[i][:], in_=theta[P * i : P * (i + 1), :])
 
             nc.vector.memset(table[:], 0.0)
             nc.scalar.activation(out=table[:], in_=table[:], func=COPY, scale=1.0)
             make_identity(nc, ident[:])
 
             interleave_grad(vector, 0, 0, 256)
-            interleave_grad(vector, 0, 256, 384)
-            interleave_grad(scalar, 0, 384, GROUP)
+            interleave_grad(vector, 0, 256, VECTOR_FIRST)
+            interleave_grad(scalar, 0, VECTOR_FIRST, GROUP)
             quantize(grad_mx[0], grad_lay[0], E5M2)
             interleave_g(vector, 0)
             interleave_g(scalar, 1)
@@ -246,24 +249,20 @@ def tile_nonlocalblocknd_pb_v_kernel(tc, theta_x, phi_x, g_x, f, grad_out, out_0
             quantize(g_mx, g_lay, E4M3, slice(GROUP // 2, GROUP))
             unread_bank = held_bank("unread_bank")
             keep_warm(unread_bank, 4)
-            multiply_dz(0, 0)
-            multiply_dz(0, 1)
+            for t in range(PACK):
+                multiply_dz(0, t)
             transpose_phi(0)
-            multiply_dz(0, 2)
-            multiply_dz(0, 3)
             transpose_phi(1)
             keep_warm(unread_bank, 2)
-            copy_dz(0, 0)
-            copy_dz(0, 1)
-            copy_words(("phi", 0, 0), phi_lay)
             interleave_grad(vector, 1, 0, GROUP)
-            copy_dz(0, 2)
-            copy_dz(0, 3)
-            copy_words(("phi", 0, 1), phi_lay)
+            for t in range(PACK):
+                copy_dz(0, t)
+            for half in range(2):
+                copy_words(("phi", 0, half), phi_lay)
             quantize(grad_mx[1], grad_lay[1], E5M2)
 
             for G in range(GROUPS):
-                early, between, late = VECTOR_OUT0[G - 1] if G > 0 else ((), (), ())
+                before, after = VECTOR_OUT0[G - 1] if G > 0 else ((), ())
                 if G > 0:
                     for i in range(TILES):
                         multiply_out0(G - 1, i)
@@ -277,15 +276,13 @@ def tile_nonlocalblocknd_pb_v_kernel(tc, theta_x, phi_x, g_x, f, grad_out, out_0
                     interleave_grad(vector, G + 2, 0, GROUP)
                 if G == 0:
                     quantize(phi_mx, phi_lay, E4M3)
-                for i in early:
+                for i in before:
                     finish_out0(vector, G - 1, i)
                 interleave_dz(G)
                 if G > 0:
                     for i in range(TILES):
-                        if i not in early + between + late:
+                        if i not in before + after:
                             finish_out0(scalar, G - 1, i)
-                for i in between:
-                    finish_out0(vector, G - 1, i)
                 for half in range(2):
                     copy_words(("dz", G, half), dzn_lay[G])
                 if G + 2 < GROUPS:
@@ -295,23 +292,24 @@ def tile_nonlocalblocknd_pb_v_kernel(tc, theta_x, phi_x, g_x, f, grad_out, out_0
                 for half in range(2):
                     copy_words(("theta", G, half), theta_lay[G])
                 quantize(dzm_mx[G], dzm_lay[G], E5M2)
-                for i in late:
+                for i in after:
                     finish_out0(vector, G - 1, i)
                 if G + 1 < GROUPS:
                     for t in range(PACK):
                         multiply_dz(G + 1, t)
                     for t in range(PACK):
                         copy_dz(G + 1, t)
-                quantize(theta_mx[G], theta_lay[G], E4M3)
                 quantize(dzn_mx[G], dzn_lay[G], E5M2)
+                quantize(theta_mx[G], theta_lay[G], E4M3)
 
+            for G in range(LAST):
+                multiply_out1(2, G)
             for i in range(TILES):
                 multiply_out0(LAST, i)
             for i in range(TILES):
                 finish_out0(vector if i in VECTOR_OUT0_LAST else scalar, LAST, i)
-            for i in range(HELD_BANKS, TILES):
-                for G in range(LAST):
-                    multiply_out1(i, G)
+            for G in range(LAST):
+                multiply_out1(3, G)
             for i in range(TILES):
                 multiply_out1(i, LAST)
             for i in range(TILES):

from contextlib import ExitStack

import concourse.mybir as mybir
from concourse.masks import make_identity

D, N, M = 512, 2048, 512

FLOPS = 3 * 2 * N * M * D
BYTES = 2 * (2 * D * N + 2 * D * M) + 4 * (D * N + D * M)

F32 = mybir.dt.float32
BF16 = mybir.dt.bfloat16
U32 = mybir.dt.uint32
U8 = mybir.dt.uint8
E4M3 = mybir.dt.float8_e4m3fn_x4
E5M2 = mybir.dt.float8_e5m2_x4
COPY = mybir.ActivationFunctionType.Copy
MULT = mybir.AluOpType.mult

P = 128
PACK = 4
GROUP = P * PACK
GROUPS = N // GROUP
LAST = GROUPS - 1
TILES = D // P
HALF = PACK * GROUP // 2
WORDS = GROUP // 2

HELD_BANKS = 2
SHARED_BANKS = 8 - HELD_BANKS

VECTOR_DZ = ((3,), (), (0, 2), (2,))
VECTOR_WORDS = (("dz", 2, 1), ("theta", 2, 0), ("dz", 3, 1))
VECTOR_OUT0 = (((2,), ()), ((), ()), ((), (1,)))
VECTOR_OUT0_LAST = (2, 3)
VECTOR_OUT1 = (2,)
VECTOR_FIRST = 448


def tile_nonlocalblocknd_pb_v_kernel(tc, theta_x, phi_x, g_x, f, grad_out, out_0, out_1):
    nc = tc.nc
    vector, scalar = nc.vector, nc.scalar
    theta, phi, g, grad = theta_x[0], phi_x[0], g_x[0], grad_out[0]
    dtheta, dphi = out_0[0], out_1[0]

    with ExitStack() as ctx:
        sb = ctx.enter_context(tc.tile_pool(name="sb", bufs=1))
        ps = ctx.enter_context(tc.psum_pool(name="ps", bufs=1))

        def sbuf(name, shape, dtype):
            return sb.tile(shape, dtype, name=name, tag=name, bufs=1, align_bytes=64)

        def shared_bank(name, shape):
            return ps.tile(shape, F32, name=name, tag="shared", bufs=SHARED_BANKS)

        def held_bank(name):
            return ps.tile([P, GROUP], F32, name=name, tag="held", bufs=HELD_BANKS)

        def mx_tiles(name):
            return sbuf(name + "_codes", [P, GROUP], U32), sbuf(name + "_scales", [P, GROUP], U8)

        def four(make, name, *args):
            return [make("%s%d" % (name, i), *args) for i in range(TILES)]

        operand = [P, PACK * GROUP]

        grad_raw = four(sbuf, "grad_raw", [P, PACK, GROUP], BF16)
        g_raw = sbuf("g_raw", [P, PACK, M], BF16)
        phi_raw = sbuf("phi_raw", [P, TILES, M], BF16)
        theta_raw = four(sbuf, "theta_raw", [P, N], BF16)
        dz = four(sbuf, "dz", [P, PACK, GROUP], BF16)
        grad_lay, grad_mx = four(sbuf, "grad_lay", operand, BF16), four(mx_tiles, "grad")
        g_lay, g_mx = sbuf("g_lay", operand, BF16), mx_tiles("g")
        phi_lay, phi_mx = sbuf("phi_lay", operand, BF16), mx_tiles("phi")
        theta_lay, theta_mx = four(sbuf, "theta_lay", operand, BF16), four(mx_tiles, "theta")
        dzm_lay, dzm_mx = four(sbuf, "dzm_lay", operand, BF16), four(mx_tiles, "dzm")
        dzn_lay, dzn_mx = four(sbuf, "dzn_lay", operand, BF16), four(mx_tiles, "dzn")
        out0_sb = four(sbuf, "out0_sb", [P, TILES, GROUP], F32)
        out1_sb = sbuf("out1_sb", [P, TILES, M], F32)

        ident = sbuf("ident", [P, P], F32)
        table = sbuf("table", [P, 1], F32)

        dz_bank, word_bank, out0_bank, out1_bank = {}, {}, {}, {}


        def copy(engine, out, in_):
            if engine is vector:
                nc.vector.tensor_copy(out=out, in_=in_)
            else:
                nc.scalar.copy(out=out, in_=in_)

        def quantize(mx, lay, fmt, cols=slice(0, GROUP)):
            codes, scales = mx
            nc.vector.quantize_mx(
                out=codes[:, cols].bitcast(fmt),
                scales=scales[:, cols],
                in_=lay[:, PACK * cols.start : PACK * cols.stop],
            )

        def multiply(out, still, i, moving, start, stop):
            cols = slice(P * i, P * (i + 1))
            nc.tensor.matmul_mx(
                out=out[:],
                lhsT=still[0][:, cols].bitcast(E4M3),
                lhsT_scale=still[1][:, cols],
                rhs=moving[0][:].bitcast(E5M2),
                rhs_scale=moving[1][:],
                start=start,
                stop=stop,
            )


        def load_grad(G, first, last):
            cols = grad[:, GROUP * G + first : GROUP * G + last]
            nc.sync.dma_start(
                out=grad_raw[G][:, :, first:last], in_=cols.rearrange("(p j) n -> p j n", j=PACK)
            )

        def interleave_grad(engine, G, first, last):
            copy(
                engine,
                grad_lay[G][:, PACK * first : PACK * last].rearrange("p (w i j) -> p w j i", i=4, j=PACK),
                grad_raw[G][:, :, first:last].rearrange("p j (w i) -> p w j i", i=4),
            )

        def interleave_g(engine, half):
            copy(
                engine,
                g_lay[:, HALF * half : HALF * (half + 1)].rearrange("p (t q j) -> p t q j", t=2, j=PACK),
                g_raw[:].rearrange("p j (q t) -> p t q j", t=PACK)[:, 2 * half : 2 * half + 2, :, :],
            )

        def multiply_dz(G, t):
            dz_bank[G, t] = shared_bank("dz_bank%d_%d" % (G, t), [P, GROUP])
            multiply(dz_bank[G, t], g_mx, t, grad_mx[G], True, True)

        def copy_dz(G, t):
            out = dz[G][:, t, :].rearrange("q (u p e) -> q u p e", u=2, e=2)
            in_ = dz_bank[G, t][:].rearrange("q (p u e) -> q u p e", u=2, e=2)
            if t in VECTOR_DZ[G]:
                nc.vector.tensor_scalar(out=out, in0=in_, scalar1=1.0 / M, scalar2=None, op0=MULT)
            else:
                nc.scalar.activation(out=out, in_=in_, func=COPY, scale=1.0 / M)

        def interleave_dz(G):
            nc.vector.tensor_copy(
                out=dzm_lay[G][:].rearrange("q (c i t) -> q c t i", i=4, t=PACK),
                in_=dz[G][:].rearrange("q t (c i) -> q c t i", i=4),
            )


        def transpose_words(key, blocks):
            bank = shared_bank("words_%s_%d_%d" % key, [P, 2, 2, P])
            for b, pair in enumerate(blocks):
                for u in range(2):
                    nc.tensor.transpose(bank[:, b, u, :], pair[u], ident[:])
            word_bank[key] = bank

        def copy_words(key, lay):
            half = key[2]
            copy(
                vector if key in VECTOR_WORDS else scalar,
                lay[:, HALF * half : HALF * (half + 1)]
                .bitcast(F32)
                .rearrange("p (b c u) -> p b c u", b=2, u=2),
                word_bank[key][:].rearrange("p b u c -> p b c u"),
            )

        def every_second_word(words, block):
            return [words[:, WORDS * block + u : WORDS * (block + 1) : 2] for u in range(2)]

        def transpose_phi(half):
            transpose_words(
                ("phi", 0, half),
                [every_second_word(phi_raw[:, 2 * half + b, :].bitcast(F32), 0) for b in range(2)],
            )

        def transpose_theta(i, half):
            transpose_words(
                ("theta", i, half),
                [every_second_word(theta_raw[i][:].bitcast(F32), 2 * half + b) for b in range(2)],
            )

        def transpose_dz(G, half):
            blocks = []
            for b in range(2):
                words = dz[G][:, 2 * half + b, :].bitcast(F32)
                blocks.append([words[:, P * u : P * (u + 1)] for u in range(2)])
            transpose_words(("dz", G, half), blocks)


        def multiply_out0(G, i):
            out0_bank[G, i] = shared_bank("out0_bank%d_%d" % (G, i), [P, GROUP])
            multiply(out0_bank[G, i], phi_mx, i, dzm_mx[G], True, True)

        def finish_out0(engine, G, i):
            copy(
                engine,
                out0_sb[G][:, i, :].rearrange("d (p u e) -> d p u e", u=2, e=2),
                out0_bank[G, i][:].rearrange("d (u p e) -> d p u e", u=2, e=2),
            )
            nc.sync.dma_start(
                out=dtheta[P * i : P * (i + 1), GROUP * G : GROUP * (G + 1)], in_=out0_sb[G][:, i, :]
            )

        def multiply_out1(i, G):
            if G == 0:
                name = "out1_bank%d" % i
                out1_bank[i] = held_bank(name) if i < HELD_BANKS else shared_bank(name, [P, M])
            multiply(out1_bank[i], theta_mx[i], G, dzn_mx[G], G == 0, G == LAST)

        def finish_out1(engine, i):
            copy(
                engine,
                out1_sb[:, i, :].rearrange("d (q t) -> d q t", t=PACK),
                out1_bank[i][:].rearrange("d (t q) -> d q t", t=PACK),
            )
            nc.sync.dma_start(out=dphi[P * i : P * (i + 1), :], in_=out1_sb[:, i, :])

        def keep_warm(bank, times):
            for i in range(times):
                nc.tensor.matmul(
                    out=bank[:], lhsT=grad_raw[0][:, 0, 0:P], rhs=grad_raw[0][:, 1, :], start=True, stop=True
                )

        with tc.manual_schedule():
            load_grad(0, 0, 256)
            load_grad(0, 256, GROUP)
            nc.sync.dma_start(out=g_raw[:], in_=g.rearrange("(p j) m -> p j m", j=PACK))
            load_grad(1, 0, GROUP)
            nc.sync.dma_start(out=phi_raw[:], in_=phi.rearrange("(i p) m -> p i m", p=P))
            for i in range(TILES):
                if i + 2 < GROUPS:
                    load_grad(i + 2, 0, GROUP)
                nc.sync.dma_start(out=theta_raw[i][:], in_=theta[P * i : P * (i + 1), :])

            nc.vector.memset(table[:], 0.0)
            nc.scalar.activation(out=table[:], in_=table[:], func=COPY, scale=1.0)
            make_identity(nc, ident[:])

            interleave_grad(vector, 0, 0, 256)
            interleave_grad(vector, 0, 256, VECTOR_FIRST)
            interleave_grad(scalar, 0, VECTOR_FIRST, GROUP)
            quantize(grad_mx[0], grad_lay[0], E5M2)
            interleave_g(vector, 0)
            interleave_g(scalar, 1)
            quantize(g_mx, g_lay, E4M3, slice(0, GROUP // 2))
            quantize(g_mx, g_lay, E4M3, slice(GROUP // 2, GROUP))
            unread_bank = held_bank("unread_bank")
            keep_warm(unread_bank, 4)
            for t in range(PACK):
                multiply_dz(0, t)
            transpose_phi(0)
            transpose_phi(1)
            keep_warm(unread_bank, 2)
            interleave_grad(vector, 1, 0, GROUP)
            for t in range(PACK):
                copy_dz(0, t)
            for half in range(2):
                copy_words(("phi", 0, half), phi_lay)
            quantize(grad_mx[1], grad_lay[1], E5M2)

            for G in range(GROUPS):
                before, after = VECTOR_OUT0[G - 1] if G > 0 else ((), ())
                if G > 0:
                    for i in range(TILES):
                        multiply_out0(G - 1, i)
                transpose_dz(G, 0)
                transpose_dz(G, 1)
                for i in range(HELD_BANKS):
                    if G > i:
                        for k in range(0 if G == i + 1 else G - 1, G):
                            multiply_out1(i, k)
                if G + 2 < GROUPS:
                    interleave_grad(vector, G + 2, 0, GROUP)
                if G == 0:
                    quantize(phi_mx, phi_lay, E4M3)
                for i in before:
                    finish_out0(vector, G - 1, i)
                interleave_dz(G)
                if G > 0:
                    for i in range(TILES):
                        if i not in before + after:
                            finish_out0(scalar, G - 1, i)
                for half in range(2):
                    copy_words(("dz", G, half), dzn_lay[G])
                if G + 2 < GROUPS:
                    quantize(grad_mx[G + 2], grad_lay[G + 2], E5M2)
                for half in range(2):
                    transpose_theta(G, half)
                for half in range(2):
                    copy_words(("theta", G, half), theta_lay[G])
                quantize(dzm_mx[G], dzm_lay[G], E5M2)
                for i in after:
                    finish_out0(vector, G - 1, i)
                if G + 1 < GROUPS:
                    for t in range(PACK):
                        multiply_dz(G + 1, t)
                    for t in range(PACK):
                        copy_dz(G + 1, t)
                quantize(dzn_mx[G], dzn_lay[G], E5M2)
                quantize(theta_mx[G], theta_lay[G], E4M3)

            for G in range(LAST):
                multiply_out1(2, G)
            for i in range(TILES):
                multiply_out0(LAST, i)
            for i in range(TILES):
                finish_out0(vector if i in VECTOR_OUT0_LAST else scalar, LAST, i)
            for G in range(LAST):
                multiply_out1(3, G)
            for i in range(TILES):
                multiply_out1(i, LAST)
            for i in range(TILES):
                finish_out1(vector if i in VECTOR_OUT1 else scalar, i)
